import numpy as np
import ml_dtypes


def mxq(x, axis, fmt="e4m3"):
    dtype, down = {"e4m3": (ml_dtypes.float8_e4m3fn, 7), "e5m2": (ml_dtypes.float8_e5m2, 14)}[fmt]
    v = np.moveaxis(np.asarray(x, np.float32).astype(ml_dtypes.bfloat16).astype(np.float64), axis, -1)
    blocks = v.reshape(v.shape[:-1] + (-1, 32))
    amax = np.abs(blocks).max(-1, keepdims=True)
    byte = np.maximum(np.where(amax > 0, np.frexp(amax)[1] - 1 + 127, 0) - down, 1)
    scale = np.exp2(byte - 127.0)
    codes = (blocks / scale).astype(np.float32).astype(dtype).astype(np.float64)
    return np.moveaxis((codes * scale).reshape(v.shape), -1, axis)


WIDE = False


def mx_kscale(k):
    if not WIDE:
        return np.ones(k)
    levels = np.array([10, -10, 5, -5, 0])
    a = np.random.permutation(np.resize(levels, k // 512 * 4)).reshape(k // 512, 4)
    idx = np.arange(k)
    return np.exp2(a[idx // 512, idx % 128 // 32])


BF16 = ml_dtypes.bfloat16


def bf(x):
    return np.asarray(x, np.float32).astype(BF16)


def f64(x):
    return np.asarray(x).astype(np.float64)


E, I, O, N = 2, 256, 16384, 256


def setup_inputs():
    s = mx_kscale(O)
    return {"inputs": bf(np.random.standard_normal((E, O, N)) * s[None, :, None]),
            "weight": bf(np.random.uniform(0.0, 1.0, (E, I, O)) * 1.7 / np.sqrt(O) / s[None, None, :]),
            "expert_size": E}


def reference(inputs, weight, expert_size):
    num_experts = weight.shape[0]
    chunks = f64(inputs)[:num_experts]
    wq = mxq(f64(weight), 2, "e4m3")
    xq = mxq(chunks, 1, "e4m3")
    out = wq[None, :, :, :] @ xq[:, None, :, :]
    C = out.shape[0]
    return out.reshape(C * num_experts, weight.shape[1], inputs.shape[2])

@@ -1,0 +1,162 @@
+from contextlib import ExitStack
+
+import concourse.mybir as mybir
+from concourse.masks import make_identity
+
+F32 = mybir.dt.float32
+BF16 = mybir.dt.bfloat16
+U32 = mybir.dt.uint32
+U8 = mybir.dt.uint8
+FP8X4 = mybir.dt.float8_e4m3fn_x4
+
+P = 128
+PACK = 4
+K_PASS = P * PACK
+PAIR = 2
+
+EXPERTS = 2
+CHUNKS = 2
+ROWS = 256
+COLS = 256
+K = 16384
+PASSES = K // K_PASS
+ROW_TILES = EXPERTS * ROWS // P
+N = CHUNKS * COLS
+
+GROUP = 8
+GROUPS = PASSES // GROUP
+BANK_PASSES = 2
+BANKS = GROUP // BANK_PASSES
+
+FLOPS = 2 * EXPERTS * CHUNKS * ROWS * COLS * K
+
+
+def tile_flaxparallelexperts_k_kernel(tc, inputs, weight, expert_size, out):
+    nc = tc.nc
+    with ExitStack() as stack:
+        const = stack.enter_context(tc.tile_pool(name="const", bufs=1))
+        w_raw_pool = stack.enter_context(tc.tile_pool(name="w_raw", bufs=6))
+        x_raw_pool = stack.enter_context(tc.tile_pool(name="x_raw", bufs=8))
+        w_grouped_pool = stack.enter_context(tc.tile_pool(name="w_grouped", bufs=2))
+        x_grouped_pool = stack.enter_context(tc.tile_pool(name="x_grouped", bufs=3))
+        w_mx_pool = stack.enter_context(tc.tile_pool(name="w_mx", bufs=2 * ROW_TILES))
+        x_mx_pool = stack.enter_context(tc.tile_pool(name="x_mx", bufs=3))
+        result_pool = stack.enter_context(tc.tile_pool(name="result", bufs=ROW_TILES))
+        flip_pool = stack.enter_context(tc.psum_pool(name="flip", bufs=BANKS))
+        acc_pool = stack.enter_context(tc.psum_pool(name="acc", bufs=1))
+        stack.enter_context(tc.manual_schedule())
+
+        identity = const.tile([P, P], F32)
+        make_identity(nc, identity[:])
+
+        acc = [acc_pool.tile([P, N], F32, name="acc%d" % r) for r in range(ROW_TILES)]
+
+        def arrange_weights(group, r):
+            expert, half = divmod(r, ROWS // P)
+            raw = w_raw_pool.tile([P, GROUP * K_PASS], BF16, name="w_raw")
+            nc.sync.dma_start(
+                out=raw[:],
+                in_=weight[
+                    expert,
+                    half * P : (half + 1) * P,
+                    group * GROUP * K_PASS : (group + 1) * GROUP * K_PASS,
+                ],
+            )
+            raw_words = raw[:].bitcast(F32)
+            grouped = w_grouped_pool.tile([P, GROUP * P * PACK], BF16, name="w_grouped", align_bytes=64)
+            grouped_words = grouped[:].bitcast(F32).rearrange(
+                "p (g m u) -> p g m u", g=GROUP, u=PACK // PAIR
+            )
+            for b in range(BANKS):
+                flipped = flip_pool.tile([P, BANK_PASSES, PACK // PAIR, P], F32, name="flipped")
+                for g in range(BANK_PASSES):
+                    for u in range(PACK // PAIR):
+                        first = ((b * BANK_PASSES + g) * (PACK // PAIR) + u) * P
+                        nc.tensor.transpose(
+                            flipped[:, g, u, :], raw_words[:, first : first + P], identity[:]
+                        )
+                copy = nc.vector.tensor_copy if b == 0 else nc.scalar.copy
+                copy(
+                    out=grouped_words[:, b * BANK_PASSES : (b + 1) * BANK_PASSES, :, :],
+                    in_=flipped[:].rearrange("p g u m -> p g m u"),
+                )
+            return grouped
+
+        def quantise_weights(grouped):
+            codes = w_mx_pool.tile([P, GROUP * P], U32, name="w_codes", align_bytes=64)
+            scales = w_mx_pool.tile([P, GROUP * P], U8, name="w_scales", align_bytes=64)
+            nc.vector.quantize_mx(out=codes[:].bitcast(FP8X4), scales=scales[:], in_=grouped[:])
+            return codes, scales
+
+        def arrange_inputs(g):
+            raw = x_raw_pool.tile([P, CHUNKS, PACK, COLS], BF16, name="x_raw")
+            grouped = x_grouped_pool.tile([P, N, PACK], BF16, name="x_grouped", align_bytes=64)
+            for c in reversed(range(CHUNKS)):
+                nc.sync.dma_start(
+                    out=raw[:, c, :, :].rearrange("p (u e) n -> p u e n", e=PAIR),
+                    in_=inputs[c, g * K_PASS : (g + 1) * K_PASS, :].rearrange(
+                        "(u p e) n -> p u e n", p=P, e=PAIR
+                    ),
+                )
+            for c in range(CHUNKS):
+                copy = nc.vector.tensor_copy if c == 0 else nc.scalar.copy
+                copy(
+                    out=grouped[:, c * COLS : (c + 1) * COLS, :].rearrange(
+                        "p (a i) t -> p a t i", i=4
+                    ),
+                    in_=raw[:, c, :, :].rearrange("p t (a i) -> p a t i", i=4),
+                )
+            return grouped
+
+        def multiply(g, grouped, w_mx):
+            codes = x_mx_pool.tile([P, N], U32, name="x_codes", align_bytes=64)
+            scales = x_mx_pool.tile([P, N], U8, name="x_scales", align_bytes=64)
+            nc.vector.quantize_mx(
+                out=codes[:].bitcast(FP8X4),
+                scales=scales[:],
+                in_=grouped[:].rearrange("p n t -> p (n t)"),
+            )
+            rows = slice((g % GROUP) * P, (g % GROUP + 1) * P)
+            for r in range(ROW_TILES):
+                w_codes, w_scales = w_mx[r]
+                nc.tensor.matmul_mx(
+                    out=acc[r][:],
+                    lhsT=w_codes[:, rows].bitcast(FP8X4),
+                    lhsT_scale=w_scales[:, rows],
+                    rhs=codes[:].bitcast(FP8X4),
+                    rhs_scale=scales[:],
+                    start=(g == 0),
+                    stop=(g == PASSES - 1),
+                )
+
+        w_mx = {}
+        w_grouped = None
+        for r in range(ROW_TILES):
+            w_before = w_grouped
+            w_grouped = arrange_weights(0, r)
+            if r > 0:
+                w_mx[(0, r - 1)] = quantise_weights(w_before)
+        w_mx[(0, ROW_TILES - 1)] = quantise_weights(w_grouped)
+
+        x_grouped = None
+        for g in range(PASSES):
+            group, step = divmod(g, GROUP)
+            x_before = x_grouped
+            x_grouped = arrange_inputs(g)
+            if g > 0:
+                before = (g - 1) // GROUP
+                multiply(g - 1, x_before, [w_mx[(before, r)] for r in range(ROW_TILES)])
+            if group + 1 < GROUPS:
+                if step % 2 == 0:
+                    w_grouped = arrange_weights(group + 1, step // 2)
+                else:
+                    w_mx[(group + 1, step // 2)] = quantise_weights(w_grouped)
+        multiply(PASSES - 1, x_grouped, [w_mx[(GROUPS - 1, r)] for r in range(ROW_TILES)])
+
+        out_view = out.rearrange("(c e) (h p) n -> e h p c n", e=EXPERTS, p=P)
+        for r in range(ROW_TILES):
+            expert, half = divmod(r, ROWS // P)
+            result = result_pool.tile([P, CHUNKS, COLS], F32, name="result")
+            copy = nc.vector.tensor_copy if r % 2 == 0 else nc.scalar.copy
+            copy(out=result[:].rearrange("p c n -> p (c n)"), in_=acc[r][:])
+            nc.sync.dma_start(out=out_view[expert, half], in_=result[:])

@@ -27,6 +27,8 @@ GROUP = 8
 GROUPS = PASSES // GROUP
 BANK_PASSES = 2
 BANKS = GROUP // BANK_PASSES
+HALVES = PACK // PAIR
+W_TILES = GROUPS * ROW_TILES
 
 FLOPS = 2 * EXPERTS * CHUNKS * ROWS * COLS * K
 
@@ -40,7 +42,7 @@ def tile_flaxparallelexperts_k_kernel(tc, inputs, weight, expert_size, out):
         w_grouped_pool = stack.enter_context(tc.tile_pool(name="w_grouped", bufs=2))
         x_grouped_pool = stack.enter_context(tc.tile_pool(name="x_grouped", bufs=3))
         w_mx_pool = stack.enter_context(tc.tile_pool(name="w_mx", bufs=2 * ROW_TILES))
-        x_mx_pool = stack.enter_context(tc.tile_pool(name="x_mx", bufs=3))
+        x_mx_pool = stack.enter_context(tc.tile_pool(name="x_mx", bufs=4))
         result_pool = stack.enter_context(tc.tile_pool(name="result", bufs=ROW_TILES))
         flip_pool = stack.enter_context(tc.psum_pool(name="flip", bufs=BANKS))
         acc_pool = stack.enter_context(tc.psum_pool(name="acc", bufs=1))
@@ -51,7 +53,8 @@ def tile_flaxparallelexperts_k_kernel(tc, inputs, weight, expert_size, out):
 
         acc = [acc_pool.tile([P, N], F32, name="acc%d" % r) for r in range(ROW_TILES)]
 
-        def arrange_weights(group, r):
+        def load_weights(w):
+            group, r = divmod(w, ROW_TILES)
             expert, half = divmod(r, ROWS // P)
             raw = w_raw_pool.tile([P, GROUP * K_PASS], BF16, name="w_raw")
             nc.sync.dma_start(
@@ -62,23 +65,32 @@ def tile_flaxparallelexperts_k_kernel(tc, inputs, weight, expert_size, out):
                     group * GROUP * K_PASS : (group + 1) * GROUP * K_PASS,
                 ],
             )
+            return raw
+
+        def flip_weights(raw):
             raw_words = raw[:].bitcast(F32)
-            grouped = w_grouped_pool.tile([P, GROUP * P * PACK], BF16, name="w_grouped", align_bytes=64)
-            grouped_words = grouped[:].bitcast(F32).rearrange(
-                "p (g m u) -> p g m u", g=GROUP, u=PACK // PAIR
-            )
+            banks = []
             for b in range(BANKS):
-                flipped = flip_pool.tile([P, BANK_PASSES, PACK // PAIR, P], F32, name="flipped")
+                flipped = flip_pool.tile([P, BANK_PASSES, HALVES, P], F32, name="flipped")
                 for g in range(BANK_PASSES):
-                    for u in range(PACK // PAIR):
-                        first = ((b * BANK_PASSES + g) * (PACK // PAIR) + u) * P
+                    for u in range(HALVES):
+                        first = ((b * BANK_PASSES + g) * HALVES + u) * P
                         nc.tensor.transpose(
                             flipped[:, g, u, :], raw_words[:, first : first + P], identity[:]
                         )
+                banks.append(flipped)
+            return banks
+
+        def gather_weights(banks):
+            grouped = w_grouped_pool.tile([P, GROUP * P * PACK], BF16, name="w_grouped", align_bytes=64)
+            grouped_words = grouped[:].bitcast(F32).rearrange(
+                "p (g m u) -> p g m u", g=GROUP, u=HALVES
+            )
+            for b in range(BANKS):
                 copy = nc.vector.tensor_copy if b == 0 else nc.scalar.copy
                 copy(
                     out=grouped_words[:, b * BANK_PASSES : (b + 1) * BANK_PASSES, :, :],
-                    in_=flipped[:].rearrange("p g u m -> p g m u"),
+                    in_=banks[b][:].rearrange("p g u m -> p g m u"),
                 )
             return grouped
 
@@ -88,9 +100,8 @@ def tile_flaxparallelexperts_k_kernel(tc, inputs, weight, expert_size, out):
             nc.vector.quantize_mx(out=codes[:].bitcast(FP8X4), scales=scales[:], in_=grouped[:])
             return codes, scales
 
-        def arrange_inputs(g):
+        def load_inputs(g):
             raw = x_raw_pool.tile([P, CHUNKS, PACK, COLS], BF16, name="x_raw")
-            grouped = x_grouped_pool.tile([P, N, PACK], BF16, name="x_grouped", align_bytes=64)
             for c in reversed(range(CHUNKS)):
                 nc.sync.dma_start(
                     out=raw[:, c, :, :].rearrange("p (u e) n -> p u e n", e=PAIR),
@@ -98,6 +109,10 @@ def tile_flaxparallelexperts_k_kernel(tc, inputs, weight, expert_size, out):
                         "(u p e) n -> p u e n", p=P, e=PAIR
                     ),
                 )
+            return raw
+
+        def regroup_inputs(raw):
+            grouped = x_grouped_pool.tile([P, N, PACK], BF16, name="x_grouped", align_bytes=64)
             for c in range(CHUNKS):
                 copy = nc.vector.tensor_copy if c == 0 else nc.scalar.copy
                 copy(
@@ -108,7 +123,7 @@ def tile_flaxparallelexperts_k_kernel(tc, inputs, weight, expert_size, out):
                 )
             return grouped
 
-        def multiply(g, grouped, w_mx):
+        def quantise_inputs(grouped):
             codes = x_mx_pool.tile([P, N], U32, name="x_codes", align_bytes=64)
             scales = x_mx_pool.tile([P, N], U8, name="x_scales", align_bytes=64)
             nc.vector.quantize_mx(
@@ -116,9 +131,13 @@ def tile_flaxparallelexperts_k_kernel(tc, inputs, weight, expert_size, out):
                 scales=scales[:],
                 in_=grouped[:].rearrange("p n t -> p (n t)"),
             )
+            return codes, scales
+
+        def multiply(g, x_mx):
+            codes, scales = x_mx
             rows = slice((g % GROUP) * P, (g % GROUP + 1) * P)
             for r in range(ROW_TILES):
-                w_codes, w_scales = w_mx[r]
+                w_codes, w_scales = w_mx[(g // GROUP) * ROW_TILES + r]
                 nc.tensor.matmul_mx(
                     out=acc[r][:],
                     lhsT=w_codes[:, rows].bitcast(FP8X4),
@@ -129,29 +148,39 @@ def tile_flaxparallelexperts_k_kernel(tc, inputs, weight, expert_size, out):
                     stop=(g == PASSES - 1),
                 )
 
-        w_mx = {}
-        w_grouped = None
-        for r in range(ROW_TILES):
-            w_before = w_grouped
-            w_grouped = arrange_weights(0, r)
-            if r > 0:
-                w_mx[(0, r - 1)] = quantise_weights(w_before)
-        w_mx[(0, ROW_TILES - 1)] = quantise_weights(w_grouped)
 
-        x_grouped = None
-        for g in range(PASSES):
-            group, step = divmod(g, GROUP)
-            x_before = x_grouped
-            x_grouped = arrange_inputs(g)
-            if g > 0:
-                before = (g - 1) // GROUP
-                multiply(g - 1, x_before, [w_mx[(before, r)] for r in range(ROW_TILES)])
-            if group + 1 < GROUPS:
-                if step % 2 == 0:
-                    w_grouped = arrange_weights(group + 1, step // 2)
-                else:
-                    w_mx[(group + 1, step // 2)] = quantise_weights(w_grouped)
-        multiply(PASSES - 1, x_grouped, [w_mx[(GROUPS - 1, r)] for r in range(ROW_TILES)])
+        w_raw = {}
+        w_banks = {}
+        w_grouped = {}
+        w_mx = {}
+        for w in range(ROW_TILES + 1):
+            w_raw[w] = load_weights(w)
+        for w in range(ROW_TILES):
+            w_banks[w] = flip_weights(w_raw[w])
+            if w > 0:
+                w_mx[w - 1] = quantise_weights(w_grouped[w - 1])
+            w_grouped[w] = gather_weights(w_banks[w])
+        w_mx[ROW_TILES - 1] = quantise_weights(w_grouped[ROW_TILES - 1])
+
+        x_grouped = {}
+        x_mx = {}
+        for s in range(PASSES + 2):
+            w = ROW_TILES + s // 2
+            even = s % 2 == 0
+            if s >= 2:
+                multiply(s - 2, x_mx[s - 2])
+            if even and w < W_TILES:
+                w_banks[w] = flip_weights(w_raw[w])
+            if not even and w < W_TILES:
+                w_grouped[w] = gather_weights(w_banks[w])
+            if s < PASSES:
+                x_grouped[s] = regroup_inputs(load_inputs(s))
+            if 1 <= s <= PASSES:
+                x_mx[s - 1] = quantise_inputs(x_grouped[s - 1])
+            if even and ROW_TILES < w <= W_TILES:
+                w_mx[w - 1] = quantise_weights(w_grouped[w - 1])
+            if even and w + 1 < W_TILES:
+                w_raw[w + 1] = load_weights(w + 1)
 
         out_view = out.rearrange("(c e) (h p) n -> e h p c n", e=EXPERTS, p=P)
         for r in range(ROW_TILES):

@@ -68,15 +68,14 @@ def tile_flaxparallelexperts_k_kernel(tc, inputs, weight, expert_size, out):
             return raw
 
         def flip_weights(raw):
-            raw_words = raw[:].bitcast(F32)
+            raw_words = raw[:].bitcast(F32).rearrange("m (g p u) -> m g u p", p=P, u=HALVES)
             banks = []
             for b in range(BANKS):
                 flipped = flip_pool.tile([P, BANK_PASSES, HALVES, P], F32, name="flipped")
                 for g in range(BANK_PASSES):
                     for u in range(HALVES):
-                        first = ((b * BANK_PASSES + g) * HALVES + u) * P
                         nc.tensor.transpose(
-                            flipped[:, g, u, :], raw_words[:, first : first + P], identity[:]
+                            flipped[:, g, u, :], raw_words[:, b * BANK_PASSES + g, u, :], identity[:]
                         )
                 banks.append(flipped)
             return banks
@@ -104,9 +103,9 @@ def tile_flaxparallelexperts_k_kernel(tc, inputs, weight, expert_size, out):
             raw = x_raw_pool.tile([P, CHUNKS, PACK, COLS], BF16, name="x_raw")
             for c in reversed(range(CHUNKS)):
                 nc.sync.dma_start(
-                    out=raw[:, c, :, :].rearrange("p (u e) n -> p u e n", e=PAIR),
+                    out=raw[:, c, :, :],
                     in_=inputs[c, g * K_PASS : (g + 1) * K_PASS, :].rearrange(
-                        "(u p e) n -> p u e n", p=P, e=PAIR
+                        "(p t) n -> p t n", t=PACK
                     ),
                 )
             return raw

@@ -23,7 +23,7 @@ PASSES = K // K_PASS
 ROW_TILES = EXPERTS * ROWS // P
 N = CHUNKS * COLS
 
-GROUP = 8
+GROUP = 4
 GROUPS = PASSES // GROUP
 BANK_PASSES = 2
 BANKS = GROUP // BANK_PASSES
@@ -37,14 +37,14 @@ def tile_flaxparallelexperts_k_kernel(tc, inputs, weight, expert_size, out):
     nc = tc.nc
     with ExitStack() as stack:
         const = stack.enter_context(tc.tile_pool(name="const", bufs=1))
-        w_raw_pool = stack.enter_context(tc.tile_pool(name="w_raw", bufs=6))
+        w_raw_pool = stack.enter_context(tc.tile_pool(name="w_raw", bufs=8))
         x_raw_pool = stack.enter_context(tc.tile_pool(name="x_raw", bufs=8))
-        w_grouped_pool = stack.enter_context(tc.tile_pool(name="w_grouped", bufs=2))
+        w_grouped_pool = stack.enter_context(tc.tile_pool(name="w_grouped", bufs=3))
         x_grouped_pool = stack.enter_context(tc.tile_pool(name="x_grouped", bufs=3))
-        w_mx_pool = stack.enter_context(tc.tile_pool(name="w_mx", bufs=2 * ROW_TILES))
+        w_mx_pool = stack.enter_context(tc.tile_pool(name="w_mx", bufs=3 * ROW_TILES))
         x_mx_pool = stack.enter_context(tc.tile_pool(name="x_mx", bufs=4))
         result_pool = stack.enter_context(tc.tile_pool(name="result", bufs=ROW_TILES))
-        flip_pool = stack.enter_context(tc.psum_pool(name="flip", bufs=BANKS))
+        flip_pool = stack.enter_context(tc.psum_pool(name="flip", bufs=2 * BANKS))
         acc_pool = stack.enter_context(tc.psum_pool(name="acc", bufs=1))
         stack.enter_context(tc.manual_schedule())
 
@@ -86,8 +86,7 @@ def tile_flaxparallelexperts_k_kernel(tc, inputs, weight, expert_size, out):
                 "p (g m u) -> p g m u", g=GROUP, u=HALVES
             )
             for b in range(BANKS):
-                copy = nc.vector.tensor_copy if b == 0 else nc.scalar.copy
-                copy(
+                nc.scalar.copy(
                     out=grouped_words[:, b * BANK_PASSES : (b + 1) * BANK_PASSES, :, :],
                     in_=banks[b][:].rearrange("p g u m -> p g m u"),
                 )
@@ -110,10 +109,10 @@ def tile_flaxparallelexperts_k_kernel(tc, inputs, weight, expert_size, out):
                 )
             return raw
 
-        def regroup_inputs(raw):
+        def regroup_inputs(g, raw):
             grouped = x_grouped_pool.tile([P, N, PACK], BF16, name="x_grouped", align_bytes=64)
-            for c in range(CHUNKS):
-                copy = nc.vector.tensor_copy if c == 0 else nc.scalar.copy
+            for c in reversed(range(CHUNKS)):
+                copy = nc.scalar.copy if c == 1 and g % 4 != 3 else nc.vector.tensor_copy
                 copy(
                     out=grouped[:, c * COLS : (c + 1) * COLS, :].rearrange(
                         "p (a i) t -> p a t i", i=4
@@ -147,38 +146,27 @@ def tile_flaxparallelexperts_k_kernel(tc, inputs, weight, expert_size, out):
                     stop=(g == PASSES - 1),
                 )
 
-
-        w_raw = {}
+        w_raw = {0: load_weights(0)}
         w_banks = {}
         w_grouped = {}
         w_mx = {}
-        for w in range(ROW_TILES + 1):
-            w_raw[w] = load_weights(w)
-        for w in range(ROW_TILES):
-            w_banks[w] = flip_weights(w_raw[w])
-            if w > 0:
-                w_mx[w - 1] = quantise_weights(w_grouped[w - 1])
-            w_grouped[w] = gather_weights(w_banks[w])
-        w_mx[ROW_TILES - 1] = quantise_weights(w_grouped[ROW_TILES - 1])
-
         x_grouped = {}
         x_mx = {}
-        for s in range(PASSES + 2):
-            w = ROW_TILES + s // 2
-            even = s % 2 == 0
+        for s in range(-ROW_TILES, PASSES + 2):
+            w = s + ROW_TILES
             if s >= 2:
                 multiply(s - 2, x_mx[s - 2])
-            if even and w < W_TILES:
+            if w < W_TILES:
                 w_banks[w] = flip_weights(w_raw[w])
-            if not even and w < W_TILES:
-                w_grouped[w] = gather_weights(w_banks[w])
-            if s < PASSES:
-                x_grouped[s] = regroup_inputs(load_inputs(s))
-            if 1 <= s <= PASSES:
+            if 0 <= w - 1 < W_TILES:
+                w_grouped[w - 1] = gather_weights(w_banks[w - 1])
+            if 0 <= s < PASSES:
+                x_grouped[s] = regroup_inputs(s, load_inputs(s))
+            if 0 <= s - 1 < PASSES:
                 x_mx[s - 1] = quantise_inputs(x_grouped[s - 1])
-            if even and ROW_TILES < w <= W_TILES:
-                w_mx[w - 1] = quantise_weights(w_grouped[w - 1])
-            if even and w + 1 < W_TILES:
+            if 0 <= w - 2 < W_TILES:
+                w_mx[w - 2] = quantise_weights(w_grouped[w - 2])
+            if w + 1 < W_TILES:
                 w_raw[w + 1] = load_weights(w + 1)
 
         out_view = out.rearrange("(c e) (h p) n -> e h p c n", e=EXPERTS, p=P)

from contextlib import ExitStack

import concourse.mybir as mybir
from concourse.masks import make_identity

F32 = mybir.dt.float32
BF16 = mybir.dt.bfloat16
U32 = mybir.dt.uint32
U8 = mybir.dt.uint8
FP8X4 = mybir.dt.float8_e4m3fn_x4

P = 128
PACK = 4
K_PASS = P * PACK
PAIR = 2

EXPERTS = 2
CHUNKS = 2
ROWS = 256
COLS = 256
K = 16384
PASSES = K // K_PASS
ROW_TILES = EXPERTS * ROWS // P
N = CHUNKS * COLS

GROUP = 4
GROUPS = PASSES // GROUP
BANK_PASSES = 2
BANKS = GROUP // BANK_PASSES
HALVES = PACK // PAIR
W_TILES = GROUPS * ROW_TILES

FLOPS = 2 * EXPERTS * CHUNKS * ROWS * COLS * K


def tile_flaxparallelexperts_k_kernel(tc, inputs, weight, expert_size, out):
    nc = tc.nc
    with ExitStack() as stack:
        const = stack.enter_context(tc.tile_pool(name="const", bufs=1))
        w_raw_pool = stack.enter_context(tc.tile_pool(name="w_raw", bufs=8))
        x_raw_pool = stack.enter_context(tc.tile_pool(name="x_raw", bufs=8))
        w_grouped_pool = stack.enter_context(tc.tile_pool(name="w_grouped", bufs=3))
        x_grouped_pool = stack.enter_context(tc.tile_pool(name="x_grouped", bufs=3))
        w_mx_pool = stack.enter_context(tc.tile_pool(name="w_mx", bufs=3 * ROW_TILES))
        x_mx_pool = stack.enter_context(tc.tile_pool(name="x_mx", bufs=4))
        result_pool = stack.enter_context(tc.tile_pool(name="result", bufs=ROW_TILES))
        flip_pool = stack.enter_context(tc.psum_pool(name="flip", bufs=2 * BANKS))
        acc_pool = stack.enter_context(tc.psum_pool(name="acc", bufs=1))
        stack.enter_context(tc.manual_schedule())

        identity = const.tile([P, P], F32)
        make_identity(nc, identity[:])

        acc = [acc_pool.tile([P, N], F32, name="acc%d" % r) for r in range(ROW_TILES)]

        def load_weights(w):
            group, r = divmod(w, ROW_TILES)
            expert, half = divmod(r, ROWS // P)
            raw = w_raw_pool.tile([P, GROUP * K_PASS], BF16, name="w_raw")
            nc.sync.dma_start(
                out=raw[:],
                in_=weight[
                    expert,
                    half * P : (half + 1) * P,
                    group * GROUP * K_PASS : (group + 1) * GROUP * K_PASS,
                ],
            )
            return raw

        def flip_weights(raw):
            raw_words = raw[:].bitcast(F32).rearrange("m (g p u) -> m g u p", p=P, u=HALVES)
            banks = []
            for b in range(BANKS):
                flipped = flip_pool.tile([P, BANK_PASSES, HALVES, P], F32, name="flipped")
                for g in range(BANK_PASSES):
                    for u in range(HALVES):
                        nc.tensor.transpose(
                            flipped[:, g, u, :], raw_words[:, b * BANK_PASSES + g, u, :], identity[:]
                        )
                banks.append(flipped)
            return banks

        def gather_weights(banks):
            grouped = w_grouped_pool.tile([P, GROUP * P * PACK], BF16, name="w_grouped", align_bytes=64)
            grouped_words = grouped[:].bitcast(F32).rearrange(
                "p (g m u) -> p g m u", g=GROUP, u=HALVES
            )
            for b in range(BANKS):
                nc.scalar.copy(
                    out=grouped_words[:, b * BANK_PASSES : (b + 1) * BANK_PASSES, :, :],
                    in_=banks[b][:].rearrange("p g u m -> p g m u"),
                )
            return grouped

        def quantise_weights(grouped):
            codes = w_mx_pool.tile([P, GROUP * P], U32, name="w_codes", align_bytes=64)
            scales = w_mx_pool.tile([P, GROUP * P], U8, name="w_scales", align_bytes=64)
            nc.vector.quantize_mx(out=codes[:].bitcast(FP8X4), scales=scales[:], in_=grouped[:])
            return codes, scales

        def load_inputs(g):
            raw = x_raw_pool.tile([P, CHUNKS, PACK, COLS], BF16, name="x_raw")
            for c in reversed(range(CHUNKS)):
                nc.sync.dma_start(
                    out=raw[:, c, :, :],
                    in_=inputs[c, g * K_PASS : (g + 1) * K_PASS, :].rearrange(
                        "(p t) n -> p t n", t=PACK
                    ),
                )
            return raw

        def regroup_inputs(g, raw):
            grouped = x_grouped_pool.tile([P, N, PACK], BF16, name="x_grouped", align_bytes=64)
            for c in reversed(range(CHUNKS)):
                copy = nc.scalar.copy if c == 1 and g % 4 != 3 else nc.vector.tensor_copy
                copy(
                    out=grouped[:, c * COLS : (c + 1) * COLS, :].rearrange(
                        "p (a i) t -> p a t i", i=4
                    ),
                    in_=raw[:, c, :, :].rearrange("p t (a i) -> p a t i", i=4),
                )
            return grouped

        def quantise_inputs(grouped):
            codes = x_mx_pool.tile([P, N], U32, name="x_codes", align_bytes=64)
            scales = x_mx_pool.tile([P, N], U8, name="x_scales", align_bytes=64)
            nc.vector.quantize_mx(
                out=codes[:].bitcast(FP8X4),
                scales=scales[:],
                in_=grouped[:].rearrange("p n t -> p (n t)"),
            )
            return codes, scales

        def multiply(g, x_mx):
            codes, scales = x_mx
            rows = slice((g % GROUP) * P, (g % GROUP + 1) * P)
            for r in range(ROW_TILES):
                w_codes, w_scales = w_mx[(g // GROUP) * ROW_TILES + r]
                nc.tensor.matmul_mx(
                    out=acc[r][:],
                    lhsT=w_codes[:, rows].bitcast(FP8X4),
                    lhsT_scale=w_scales[:, rows],
                    rhs=codes[:].bitcast(FP8X4),
                    rhs_scale=scales[:],
                    start=(g == 0),
                    stop=(g == PASSES - 1),
                )

        w_raw = {0: load_weights(0)}
        w_banks = {}
        w_grouped = {}
        w_mx = {}
        x_grouped = {}
        x_mx = {}
        for s in range(-ROW_TILES, PASSES + 2):
            w = s + ROW_TILES
            if s >= 2:
                multiply(s - 2, x_mx[s - 2])
            if w < W_TILES:
                w_banks[w] = flip_weights(w_raw[w])
            if 0 <= w - 1 < W_TILES:
                w_grouped[w - 1] = gather_weights(w_banks[w - 1])
            if 0 <= s < PASSES:
                x_grouped[s] = regroup_inputs(s, load_inputs(s))
            if 0 <= s - 1 < PASSES:
                x_mx[s - 1] = quantise_inputs(x_grouped[s - 1])
            if 0 <= w - 2 < W_TILES:
                w_mx[w - 2] = quantise_weights(w_grouped[w - 2])
            if w + 1 < W_TILES:
                w_raw[w + 1] = load_weights(w + 1)

        out_view = out.rearrange("(c e) (h p) n -> e h p c n", e=EXPERTS, p=P)
        for r in range(ROW_TILES):
            expert, half = divmod(r, ROWS // P)
            result = result_pool.tile([P, CHUNKS, COLS], F32, name="result")
            copy = nc.vector.tensor_copy if r % 2 == 0 else nc.scalar.copy
            copy(out=result[:].rearrange("p c n -> p (c n)"), in_=acc[r][:])
            nc.sync.dma_start(out=out_view[expert, half], in_=result[:])
